import numpy as np
import ml_dtypes


def mxq(x, axis, fmt="e4m3"):
    dtype, down = {"e4m3": (ml_dtypes.float8_e4m3fn, 7), "e5m2": (ml_dtypes.float8_e5m2, 14)}[fmt]
    v = np.moveaxis(np.asarray(x, np.float32).astype(ml_dtypes.bfloat16).astype(np.float64), axis, -1)
    blocks = v.reshape(v.shape[:-1] + (-1, 32))
    amax = np.abs(blocks).max(-1, keepdims=True)
    byte = np.maximum(np.where(amax > 0, np.frexp(amax)[1] - 1 + 127, 0) - down, 1)
    scale = np.exp2(byte - 127.0)
    codes = (blocks / scale).astype(np.float32).astype(dtype).astype(np.float64)
    return np.moveaxis((codes * scale).reshape(v.shape), -1, axis)


WIDE = False


def mx_kscale(k):
    if not WIDE:
        return np.ones(k)
    levels = np.array([10, -10, 5, -5, 0])
    a = np.random.permutation(np.resize(levels, k // 512 * 4)).reshape(k // 512, 4)
    idx = np.arange(k)
    return np.exp2(a[idx // 512, idx % 128 // 32])


BF16 = ml_dtypes.bfloat16


def bf(x):
    return np.asarray(x, np.float32).astype(BF16)


def f64(x):
    return np.asarray(x).astype(np.float64)


S, D, DA, FF = 256, 2048, 2048, 2560
HALF = DA // 2
EPS = 1.1920929e-07
ROPE_BASE = 10000.0


def rms_norm(x, w):
    return x * (1.0 / np.sqrt(np.mean(x * x, axis=-1, keepdims=True) + EPS)) * w


def rope(y, cos, sin):
    y1, y2 = y[:, :HALF], y[:, HALF:]
    return np.concatenate([y1 * cos - y2 * sin, y1 * sin + y2 * cos], axis=-1)


def setup_inputs():
    s = mx_kscale(D)
    angles = np.outer(np.arange(S), 1.0 / ROPE_BASE ** (np.arange(0, DA, 2) / DA))
    return {"x": bf(np.random.standard_normal((S, D))),
            "w_rn1": bf((1.0 + 0.1 * np.random.standard_normal(D)) * s),
            "wq": bf(np.random.standard_normal((DA, D)) / np.sqrt(D) / s[None, :]),
            "wk": bf(np.random.standard_normal((DA, D)) / np.sqrt(D) / s[None, :]),
            "wv": bf(np.random.standard_normal((DA, D)) * 2.0 / np.sqrt(D) / s[None, :]),
            "cos": bf(np.cos(angles)),
            "sin": bf(np.sin(angles))}


def reference(x, w_rn1, wq, wk, wv, cos, sin):
    h = mxq(rms_norm(f64(x), f64(w_rn1)), 1, "e4m3")
    c, sn = f64(cos), f64(sin)
    q = rope(h @ mxq(f64(wq), 1, "e4m3").T, c, sn)
    k = rope(h @ mxq(f64(wk), 1, "e4m3").T, c, sn)
    v = h @ mxq(f64(wv), 1, "e4m3").T
    return q, k, v

@@ -1,0 +1,266 @@
+from contextlib import ExitStack
+
+import concourse.mybir as mybir
+from concourse.masks import make_identity
+
+BF16 = mybir.dt.bfloat16
+F32 = mybir.dt.float32
+U32 = mybir.dt.uint32
+U8 = mybir.dt.uint8
+FP8X4 = mybir.dt.float8_e4m3fn_x4
+ACT = mybir.ActivationFunctionType
+ALU = mybir.AluOpType
+
+P = 128
+S = 256
+D = 2048
+DA = 2048
+HALF = DA // 2
+EPS = 1.1920929e-07
+
+ROW_TILES = S // P
+K_PASS = 4 * P
+PASSES = D // K_PASS
+PASS_WORDS = K_PASS // 2
+ROW_WORDS = D // 2
+
+UNIT = 512
+UNIT_TILES = UNIT // P
+UNITS = 3 * DA // UNIT
+GROUP_UNITS = 3
+BANK = 512
+
+STEP_PASSES = 2
+UNIT_STEPS = PASSES // STEP_PASSES
+STEPS = UNITS * UNIT_STEPS
+STEP_BANKS = 4
+PRODUCTS = UNITS * ROW_TILES
+
+RAW_BUFS = 4
+PASS_LAG = 3
+
+FLOPS = 2 * S * D * 3 * DA
+
+
+def tile_llamablock_pa_kernel(tc, x, w_rn1, wq, wk, wv, cos, sin, out_0, out_1, out_2):
+    nc = tc.nc
+
+    units = []
+    for group in range(UNITS // GROUP_UNITS):
+        w_rot, out_rot = (wq, out_0) if group < 2 else (wk, out_1)
+        col = UNIT * (group % 2)
+        units.append((w_rot, out_rot, col))
+        units.append((w_rot, out_rot, HALF + col))
+        units.append((wv, out_2, UNIT * group))
+
+    with ExitStack() as ctx:
+        keep = ctx.enter_context(tc.tile_pool(name="keep", bufs=1))
+        raw_pool = ctx.enter_context(tc.tile_pool(name="raw", bufs=RAW_BUFS))
+        grouped_pool = ctx.enter_context(tc.tile_pool(name="grouped", bufs=3))
+        mx_pool = ctx.enter_context(tc.tile_pool(name="mx", bufs=3))
+        rope_pool = ctx.enter_context(tc.tile_pool(name="rope", bufs=3))
+        flip_psum = ctx.enter_context(tc.psum_pool(name="flip", bufs=STEP_BANKS))
+        acc_psum = ctx.enter_context(tc.psum_pool(name="acc", bufs=4))
+        ctx.enter_context(tc.manual_schedule())
+
+        raw_of = {}
+        grouped_of = {}
+        codes_of = {}
+        scales_of = {}
+        acc_of = {}
+        rot = {}
+
+        def load_unit(i):
+            w_dram, row = units[i][0], units[i][2]
+            raw = raw_pool.tile([P, UNIT_TILES * D], BF16)
+            nc.sync.dma_start(
+                out=raw[:].rearrange("p (t k) -> p t k", t=UNIT_TILES),
+                in_=w_dram[row : row + UNIT, :].rearrange("(t p) k -> p t k", p=P),
+            )
+            raw_of[i] = raw
+
+        eps = keep.tile([P, 1], F32)
+        nc.vector.memset(eps[:], EPS)
+        gain_rows = keep.tile([P, 2 * P], BF16)
+        nc.vector.memset(gain_rows[:], 0.0)
+        ones = keep.tile([P, P], F32)
+        nc.vector.memset(ones[:], 1.0)
+        ident = keep.tile([P, P], F32)
+        make_identity(nc, ident[:])
+        warm = keep.tile([P, 1], F32)
+        nc.scalar.activation(out=warm[:], in_=eps[:], func=ACT.Sqrt)
+
+        x_sb = keep.tile([P, ROW_TILES * D], BF16)
+        for m in range(ROW_TILES):
+            nc.sync.dma_start(out=x_sb[:, m * D : (m + 1) * D], in_=x[m * P : (m + 1) * P, :])
+        nc.scalar.dma_start(
+            out=gain_rows[0 : D // (2 * P), :], in_=w_rn1.rearrange("(a c) -> a c", c=2 * P)
+        )
+        cos_sb = keep.tile([P, ROW_TILES * HALF], BF16)
+        sin_sb = keep.tile([P, ROW_TILES * HALF], BF16)
+        for i in range(RAW_BUFS):
+            load_unit(i)
+            if i == RAW_BUFS - 2:
+                for table, table_sb in ((cos, cos_sb), (sin, sin_sb)):
+                    nc.sync.dma_start(
+                        out=table_sb[:].rearrange("p (m j) -> p m j", m=ROW_TILES),
+                        in_=table.rearrange("(m p) j -> p m j", p=P),
+                    )
+
+        gain_t = acc_psum.tile([P, BANK], F32, tag="acc")
+        nc.tensor.transpose(out=gain_t[:, 0:P], in_=gain_rows[:].bitcast(F32), identity=ident[:])
+        gain4 = keep.tile([P, 2 * PASSES], F32)
+        nc.vector.tensor_copy(out=gain4[:], in_=gain_t[:, 0 : 2 * PASSES])
+        gain4_bf = gain4[:].bitcast(BF16)
+
+        sumsq = keep.tile([P, ROW_TILES], F32)
+        for m in range(ROW_TILES):
+            squares = keep.tile([P, D], BF16, name="squares%d" % m)
+            nc.scalar.activation(
+                out=squares[:],
+                in_=x_sb[:, m * D : (m + 1) * D],
+                func=ACT.Square,
+                accum_out=sumsq[:, m : m + 1],
+            )
+
+        x_words = x_sb[:].bitcast(F32)
+        xg = keep.tile([P, PASSES * S * 4], F32)
+        for g in range(PASSES):
+            x_t = acc_psum.tile([P, BANK], F32, tag="acc")
+            for u in range(2):
+                for m in range(ROW_TILES):
+                    first = m * ROW_WORDS + g * PASS_WORDS + u * P
+                    nc.tensor.transpose(
+                        out=x_t[:, u * S + m * P : u * S + (m + 1) * P],
+                        in_=x_words[:, first : first + P],
+                        identity=ident[:],
+                    )
+            nc.vector.tensor_tensor(
+                out=xg[:, g * S * 4 : (g + 1) * S * 4].rearrange("p (s u e) -> p s u e", u=2, e=2),
+                in0=x_t[:].bitcast(BF16).rearrange("p (u s e) -> p s u e", u=2, e=2),
+                in1=gain4_bf[:, 4 * g : 4 * g + 4]
+                .rearrange("p (o u e) -> p o u e", o=1, u=2)
+                .to_broadcast([P, S, 2, 2]),
+                op=ALU.mult,
+            )
+
+        std = keep.tile([P, ROW_TILES], F32)
+        nc.scalar.activation(out=std[:], in_=sumsq[:], func=ACT.Sqrt, bias=eps[:], scale=1.0 / D)
+        rstd = keep.tile([P, ROW_TILES], F32)
+        nc.vector.reciprocal(out=rstd[:], in_=std[:])
+        rstd_rep = keep.tile([P, S], F32)
+        rstd_t = acc_psum.tile([P, BANK], F32, tag="acc")
+        for m in range(ROW_TILES):
+            nc.vector.tensor_scalar_mul(
+                out=rstd_rep[:, m * P : (m + 1) * P], in0=ones[:], scalar1=rstd[:, m : m + 1]
+            )
+            nc.tensor.transpose(
+                out=rstd_t[:, m * P : (m + 1) * P],
+                in_=rstd_rep[:, m * P : (m + 1) * P],
+                identity=ident[:],
+            )
+
+        h_grouped = keep.tile([P, PASSES * S * 4], BF16, align_bytes=64)
+        for g in range(PASSES):
+            nc.vector.tensor_tensor(
+                out=h_grouped[:, g * S * 4 : (g + 1) * S * 4].rearrange("p (s t) -> p s t", t=4),
+                in0=xg[:, g * S * 4 : (g + 1) * S * 4].rearrange("p (s t) -> p s t", t=4),
+                in1=rstd_t[:, 0:S].unsqueeze(2).to_broadcast([P, S, 4]),
+                op=ALU.mult,
+            )
+        h_codes = keep.tile([P, PASSES * S], U32, align_bytes=64)
+        h_scales = keep.tile([P, PASSES * S], U8, align_bytes=64)
+        nc.vector.quantize_mx(out=h_codes[:].bitcast(FP8X4), scales=h_scales[:], in_=h_grouped[:])
+
+        def transpose_step(s):
+            i, half = divmod(s, UNIT_STEPS)
+            raw_words = raw_of[i][:].bitcast(F32)
+            grouped = grouped_pool.tile([P, STEP_PASSES * UNIT * 4], BF16, align_bytes=64)
+            grouped_words = grouped[:].bitcast(F32).rearrange("p (b n u) -> p b n u", b=STEP_BANKS, u=2)
+            for b in range(STEP_BANKS):
+                g = half * STEP_PASSES + b // 2
+                flipped = flip_psum.tile([P, BANK], F32)
+                for u in range(2):
+                    for j in range(2):
+                        t = 2 * (b % 2) + j
+                        first = t * ROW_WORDS + g * PASS_WORDS + u * P
+                        nc.tensor.transpose(
+                            out=flipped[:, (2 * u + j) * P : (2 * u + j + 1) * P],
+                            in_=raw_words[:, first : first + P],
+                            identity=ident[:],
+                        )
+                nc.scalar.copy(
+                    out=grouped_words[:, b], in_=flipped[:].rearrange("p (u n) -> p n u", u=2)
+                )
+            grouped_of[s] = grouped
+
+        def quantise_step(s):
+            i, half = divmod(s, UNIT_STEPS)
+            if half == 0:
+                codes = mx_pool.tile([P, PASSES * UNIT], U32, align_bytes=64)
+                scales = mx_pool.tile([P, PASSES * UNIT], U8, align_bytes=64)
+                codes_of[i] = codes
+                scales_of[i] = scales
+            cols = slice(half * STEP_PASSES * UNIT, (half + 1) * STEP_PASSES * UNIT)
+            nc.vector.quantize_mx(
+                out=codes_of[i][:, cols].bitcast(FP8X4),
+                scales=scales_of[i][:, cols],
+                in_=grouped_of[s][:],
+            )
+
+        def multiply(n):
+            i, m = divmod(n, ROW_TILES)
+            acc = acc_psum.tile([P, BANK], F32, tag="acc")
+            for g in range(PASSES):
+                rows = slice(g * S + m * P, g * S + (m + 1) * P)
+                cols = slice(g * UNIT, (g + 1) * UNIT)
+                nc.tensor.matmul_mx(
+                    out=acc[:],
+                    lhsT=h_codes[:, rows].bitcast(FP8X4),
+                    lhsT_scale=h_scales[:, rows],
+                    rhs=codes_of[i][:, cols].bitcast(FP8X4),
+                    rhs_scale=scales_of[i][:, cols],
+                    start=(g == 0),
+                    stop=(g == PASSES - 1),
+                )
+            acc_of[n] = acc
+
+        def finish(n):
+            i, m = divmod(n, ROW_TILES)
+            out, col = units[i][1], units[i][2]
+            rows = slice(m * P, (m + 1) * P)
+            acc = acc_of[n]
+            kind = i % GROUP_UNITS
+            if kind < 2:
+                table_cols = slice(m * HALF + col % HALF, m * HALF + col % HALF + UNIT)
+                by_cos = rope_pool.tile([P, UNIT], F32, name="by_cos%d" % kind)
+                by_sin = rope_pool.tile([P, UNIT], F32, name="by_sin%d" % kind)
+                nc.vector.tensor_tensor(out=by_cos[:], in0=acc[:], in1=cos_sb[:, table_cols], op=ALU.mult)
+                nc.vector.tensor_tensor(out=by_sin[:], in0=acc[:], in1=sin_sb[:, table_cols], op=ALU.mult)
+                rot[(kind, m)] = (by_cos, by_sin)
+            else:
+                v_sb = rope_pool.tile([P, UNIT], F32)
+                nc.scalar.copy(out=v_sb[:], in_=acc[:])
+                nc.gpsimd.dma_start(out=out[rows, col : col + UNIT], in_=v_sb[:])
+                out_rot, col_rot = units[i - 2][1], units[i - 2][2]
+                y1_cos, y1_sin = rot[(0, m)]
+                y2_cos, y2_sin = rot[(1, m)]
+                nc.vector.tensor_tensor(out=y1_cos[:], in0=y1_cos[:], in1=y2_sin[:], op=ALU.subtract)
+                nc.vector.tensor_tensor(out=y1_sin[:], in0=y1_sin[:], in1=y2_cos[:], op=ALU.add)
+                nc.gpsimd.dma_start(out=out_rot[rows, col_rot : col_rot + UNIT], in_=y1_cos[:])
+                nc.gpsimd.dma_start(
+                    out=out_rot[rows, HALF + col_rot : HALF + col_rot + UNIT], in_=y1_sin[:]
+                )
+
+        for s in range(STEPS + PASS_LAG + 1):
+            next_unit = s // UNIT_STEPS + RAW_BUFS - 1
+            if s % UNIT_STEPS == 0 and RAW_BUFS <= next_unit < UNITS:
+                load_unit(next_unit)
+            if s < STEPS:
+                transpose_step(s)
+            if 1 <= s <= STEPS:
+                quantise_step(s - 1)
+            if 0 <= s - PASS_LAG < PRODUCTS:
+                multiply(s - PASS_LAG)
+            if 0 <= s - PASS_LAG - 1 < PRODUCTS:
+                finish(s - PASS_LAG - 1)

@@ -23,21 +23,24 @@ K_PASS = 4 * P
 PASSES = D // K_PASS
 PASS_WORDS = K_PASS // 2
 ROW_WORDS = D // 2
-
-UNIT = 512
-UNIT_TILES = UNIT // P
-UNITS = 3 * DA // UNIT
-GROUP_UNITS = 3
 BANK = 512
 
-STEP_PASSES = 2
-UNIT_STEPS = PASSES // STEP_PASSES
-STEPS = UNITS * UNIT_STEPS
-STEP_BANKS = 4
+UNIT = 512
+UNITS = 3 * DA // UNIT
 PRODUCTS = UNITS * ROW_TILES
+CHUNK = 256
+CHUNK_TILES = CHUNK // P
+UNIT_CHUNKS = UNIT // CHUNK
+CHUNKS = UNITS * UNIT_CHUNKS
 
-RAW_BUFS = 4
+FIRST = 0
+SECOND = 1
+PLAIN = 2
+
+RAW_BUFS = 6
+TABLES_AFTER = 4
 PASS_LAG = 3
+SUM_LAG = 2
 
 FLOPS = 2 * S * D * 3 * DA
 
@@ -45,21 +48,26 @@ FLOPS = 2 * S * D * 3 * DA
 def tile_llamablock_pa_kernel(tc, x, w_rn1, wq, wk, wv, cos, sin, out_0, out_1, out_2):
     nc = tc.nc
 
-    units = []
-    for group in range(UNITS // GROUP_UNITS):
-        w_rot, out_rot = (wq, out_0) if group < 2 else (wk, out_1)
-        col = UNIT * (group % 2)
-        units.append((w_rot, out_rot, col))
-        units.append((w_rot, out_rot, HALF + col))
-        units.append((wv, out_2, UNIT * group))
+    def rotary_pair(w, out, col):
+        return [(w, out, col, FIRST), (w, out, HALF + col, SECOND)]
+
+    def plain(block):
+        return [(wv, out_2, block * UNIT, PLAIN)]
+
+    units = (
+        rotary_pair(wq, out_0, 0) + plain(0) + rotary_pair(wq, out_0, UNIT) + plain(1)
+        + rotary_pair(wk, out_1, 0) + rotary_pair(wk, out_1, UNIT) + plain(2) + plain(3)
+    )
 
     with ExitStack() as ctx:
         keep = ctx.enter_context(tc.tile_pool(name="keep", bufs=1))
         raw_pool = ctx.enter_context(tc.tile_pool(name="raw", bufs=RAW_BUFS))
         grouped_pool = ctx.enter_context(tc.tile_pool(name="grouped", bufs=3))
         mx_pool = ctx.enter_context(tc.tile_pool(name="mx", bufs=3))
-        rope_pool = ctx.enter_context(tc.tile_pool(name="rope", bufs=3))
-        flip_psum = ctx.enter_context(tc.psum_pool(name="flip", bufs=STEP_BANKS))
+        first_pool = ctx.enter_context(tc.tile_pool(name="first", bufs=4))
+        second_pool = ctx.enter_context(tc.tile_pool(name="second", bufs=2))
+        plain_pool = ctx.enter_context(tc.tile_pool(name="plain", bufs=3))
+        flip_psum = ctx.enter_context(tc.psum_pool(name="flip", bufs=4))
         acc_psum = ctx.enter_context(tc.psum_pool(name="acc", bufs=4))
         ctx.enter_context(tc.manual_schedule())
 
@@ -68,21 +76,23 @@ def tile_llamablock_pa_kernel(tc, x, w_rn1, wq, wk, wv, cos, sin, out_0, out_1, 
         codes_of = {}
         scales_of = {}
         acc_of = {}
-        rot = {}
+        rotated = {}
 
-        def load_unit(i):
-            w_dram, row = units[i][0], units[i][2]
-            raw = raw_pool.tile([P, UNIT_TILES * D], BF16)
+        def load_chunk(c):
+            i, part = divmod(c, UNIT_CHUNKS)
+            w_dram = units[i][0]
+            row = units[i][2] + part * CHUNK
+            raw = raw_pool.tile([P, CHUNK_TILES * D], BF16)
             nc.sync.dma_start(
-                out=raw[:].rearrange("p (t k) -> p t k", t=UNIT_TILES),
-                in_=w_dram[row : row + UNIT, :].rearrange("(t p) k -> p t k", p=P),
+                out=raw[:].rearrange("p (t k) -> p t k", t=CHUNK_TILES),
+                in_=w_dram[row : row + CHUNK, :].rearrange("(t p) k -> p t k", p=P),
             )
-            raw_of[i] = raw
+            raw_of[c] = raw
 
-        eps = keep.tile([P, 1], F32)
-        nc.vector.memset(eps[:], EPS)
         gain_rows = keep.tile([P, 2 * P], BF16)
         nc.vector.memset(gain_rows[:], 0.0)
+        eps = keep.tile([P, 1], F32)
+        nc.vector.memset(eps[:], EPS)
         ones = keep.tile([P, P], F32)
         nc.vector.memset(ones[:], 1.0)
         ident = keep.tile([P, P], F32)
@@ -90,17 +100,17 @@ def tile_llamablock_pa_kernel(tc, x, w_rn1, wq, wk, wv, cos, sin, out_0, out_1, 
         warm = keep.tile([P, 1], F32)
         nc.scalar.activation(out=warm[:], in_=eps[:], func=ACT.Sqrt)
 
+        nc.sync.dma_start(
+            out=gain_rows[0 : D // (2 * P), :], in_=w_rn1.rearrange("(a c) -> a c", c=2 * P)
+        )
         x_sb = keep.tile([P, ROW_TILES * D], BF16)
         for m in range(ROW_TILES):
             nc.sync.dma_start(out=x_sb[:, m * D : (m + 1) * D], in_=x[m * P : (m + 1) * P, :])
-        nc.scalar.dma_start(
-            out=gain_rows[0 : D // (2 * P), :], in_=w_rn1.rearrange("(a c) -> a c", c=2 * P)
-        )
         cos_sb = keep.tile([P, ROW_TILES * HALF], BF16)
         sin_sb = keep.tile([P, ROW_TILES * HALF], BF16)
-        for i in range(RAW_BUFS):
-            load_unit(i)
-            if i == RAW_BUFS - 2:
+        for c in range(RAW_BUFS):
+            load_chunk(c)
+            if c == TABLES_AFTER:
                 for table, table_sb in ((cos, cos_sb), (sin, sin_sb)):
                     nc.sync.dma_start(
                         out=table_sb[:].rearrange("p (m j) -> p m j", m=ROW_TILES),
@@ -144,69 +154,70 @@ def tile_llamablock_pa_kernel(tc, x, w_rn1, wq, wk, wv, cos, sin, out_0, out_1, 
                 op=ALU.mult,
             )
 
+        h_codes = keep.tile([P, PASSES * S], U32, align_bytes=64)
+        h_scales = keep.tile([P, PASSES * S], U8, align_bytes=64)
+
         std = keep.tile([P, ROW_TILES], F32)
         nc.scalar.activation(out=std[:], in_=sumsq[:], func=ACT.Sqrt, bias=eps[:], scale=1.0 / D)
         rstd = keep.tile([P, ROW_TILES], F32)
         nc.vector.reciprocal(out=rstd[:], in_=std[:])
         rstd_rep = keep.tile([P, S], F32)
-        rstd_t = acc_psum.tile([P, BANK], F32, tag="acc")
         for m in range(ROW_TILES):
             nc.vector.tensor_scalar_mul(
                 out=rstd_rep[:, m * P : (m + 1) * P], in0=ones[:], scalar1=rstd[:, m : m + 1]
             )
-            nc.tensor.transpose(
-                out=rstd_t[:, m * P : (m + 1) * P],
-                in_=rstd_rep[:, m * P : (m + 1) * P],
-                identity=ident[:],
-            )
 
-        h_grouped = keep.tile([P, PASSES * S * 4], BF16, align_bytes=64)
-        for g in range(PASSES):
-            nc.vector.tensor_tensor(
-                out=h_grouped[:, g * S * 4 : (g + 1) * S * 4].rearrange("p (s t) -> p s t", t=4),
-                in0=xg[:, g * S * 4 : (g + 1) * S * 4].rearrange("p (s t) -> p s t", t=4),
-                in1=rstd_t[:, 0:S].unsqueeze(2).to_broadcast([P, S, 4]),
-                op=ALU.mult,
-            )
-        h_codes = keep.tile([P, PASSES * S], U32, align_bytes=64)
-        h_scales = keep.tile([P, PASSES * S], U8, align_bytes=64)
-        nc.vector.quantize_mx(out=h_codes[:].bitcast(FP8X4), scales=h_scales[:], in_=h_grouped[:])
+        def finish_norm():
+            rstd_t = acc_psum.tile([P, BANK], F32, tag="acc")
+            for m in range(ROW_TILES):
+                nc.tensor.transpose(
+                    out=rstd_t[:, m * P : (m + 1) * P],
+                    in_=rstd_rep[:, m * P : (m + 1) * P],
+                    identity=ident[:],
+                )
+            h_grouped = keep.tile([P, PASSES * S * 4], BF16, align_bytes=64)
+            for g in range(PASSES):
+                nc.vector.tensor_tensor(
+                    out=h_grouped[:, g * S * 4 : (g + 1) * S * 4].rearrange("p (s t) -> p s t", t=4),
+                    in0=xg[:, g * S * 4 : (g + 1) * S * 4].rearrange("p (s t) -> p s t", t=4),
+                    in1=rstd_t[:, 0:S].unsqueeze(2).to_broadcast([P, S, 4]),
+                    op=ALU.mult,
+                )
+            nc.vector.quantize_mx(out=h_codes[:].bitcast(FP8X4), scales=h_scales[:], in_=h_grouped[:])
 
-        def transpose_step(s):
-            i, half = divmod(s, UNIT_STEPS)
-            raw_words = raw_of[i][:].bitcast(F32)
-            grouped = grouped_pool.tile([P, STEP_PASSES * UNIT * 4], BF16, align_bytes=64)
-            grouped_words = grouped[:].bitcast(F32).rearrange("p (b n u) -> p b n u", b=STEP_BANKS, u=2)
-            for b in range(STEP_BANKS):
-                g = half * STEP_PASSES + b // 2
+        def transpose_chunk(c):
+            raw_words = raw_of[c][:].bitcast(F32)
+            grouped = grouped_pool.tile([P, PASSES * CHUNK * 4], BF16, align_bytes=64)
+            grouped_words = grouped[:].bitcast(F32).rearrange("p (g n u) -> p g n u", g=PASSES, u=2)
+            for g in range(PASSES):
                 flipped = flip_psum.tile([P, BANK], F32)
                 for u in range(2):
-                    for j in range(2):
-                        t = 2 * (b % 2) + j
+                    for t in range(CHUNK_TILES):
                         first = t * ROW_WORDS + g * PASS_WORDS + u * P
                         nc.tensor.transpose(
-                            out=flipped[:, (2 * u + j) * P : (2 * u + j + 1) * P],
+                            out=flipped[:, u * CHUNK + t * P : u * CHUNK + (t + 1) * P],
                             in_=raw_words[:, first : first + P],
                             identity=ident[:],
                         )
                 nc.scalar.copy(
-                    out=grouped_words[:, b], in_=flipped[:].rearrange("p (u n) -> p n u", u=2)
+                    out=grouped_words[:, g], in_=flipped[:].rearrange("p (u n) -> p n u", u=2)
                 )
-            grouped_of[s] = grouped
+            grouped_of[c] = grouped
 
-        def quantise_step(s):
-            i, half = divmod(s, UNIT_STEPS)
-            if half == 0:
+        def quantise_chunk(c):
+            i, part = divmod(c, UNIT_CHUNKS)
+            if part == 0:
                 codes = mx_pool.tile([P, PASSES * UNIT], U32, align_bytes=64)
                 scales = mx_pool.tile([P, PASSES * UNIT], U8, align_bytes=64)
                 codes_of[i] = codes
                 scales_of[i] = scales
-            cols = slice(half * STEP_PASSES * UNIT, (half + 1) * STEP_PASSES * UNIT)
-            nc.vector.quantize_mx(
-                out=codes_of[i][:, cols].bitcast(FP8X4),
-                scales=scales_of[i][:, cols],
-                in_=grouped_of[s][:],
-            )
+            for g in range(PASSES):
+                cols = slice(g * UNIT + part * CHUNK, g * UNIT + (part + 1) * CHUNK)
+                nc.vector.quantize_mx(
+                    out=codes_of[i][:, cols].bitcast(FP8X4),
+                    scales=scales_of[i][:, cols],
+                    in_=grouped_of[c][:, g * CHUNK * 4 : (g + 1) * CHUNK * 4],
+                )
 
         def multiply(n):
             i, m = divmod(n, ROW_TILES)
@@ -225,42 +236,48 @@ def tile_llamablock_pa_kernel(tc, x, w_rn1, wq, wk, wv, cos, sin, out_0, out_1, 
                 )
             acc_of[n] = acc
 
-        def finish(n):
+        def empty_bank(n):
             i, m = divmod(n, ROW_TILES)
-            out, col = units[i][1], units[i][2]
-            rows = slice(m * P, (m + 1) * P)
+            out, col, kind = units[i][1], units[i][2], units[i][3]
             acc = acc_of[n]
-            kind = i % GROUP_UNITS
-            if kind < 2:
+            if kind == PLAIN:
+                v_sb = plain_pool.tile([P, UNIT], F32)
+                nc.scalar.copy(out=v_sb[:], in_=acc[:])
+                nc.sync.dma_start(out=out[m * P : (m + 1) * P, col : col + UNIT], in_=v_sb[:])
+            else:
+                pool = first_pool if kind == FIRST else second_pool
                 table_cols = slice(m * HALF + col % HALF, m * HALF + col % HALF + UNIT)
-                by_cos = rope_pool.tile([P, UNIT], F32, name="by_cos%d" % kind)
-                by_sin = rope_pool.tile([P, UNIT], F32, name="by_sin%d" % kind)
+                by_cos = pool.tile([P, UNIT], F32)
+                by_sin = pool.tile([P, UNIT], F32)
                 nc.vector.tensor_tensor(out=by_cos[:], in0=acc[:], in1=cos_sb[:, table_cols], op=ALU.mult)
                 nc.vector.tensor_tensor(out=by_sin[:], in0=acc[:], in1=sin_sb[:, table_cols], op=ALU.mult)
-                rot[(kind, m)] = (by_cos, by_sin)
-            else:
-                v_sb = rope_pool.tile([P, UNIT], F32)
-                nc.scalar.copy(out=v_sb[:], in_=acc[:])
-                nc.gpsimd.dma_start(out=out[rows, col : col + UNIT], in_=v_sb[:])
-                out_rot, col_rot = units[i - 2][1], units[i - 2][2]
-                y1_cos, y1_sin = rot[(0, m)]
-                y2_cos, y2_sin = rot[(1, m)]
-                nc.vector.tensor_tensor(out=y1_cos[:], in0=y1_cos[:], in1=y2_sin[:], op=ALU.subtract)
-                nc.vector.tensor_tensor(out=y1_sin[:], in0=y1_sin[:], in1=y2_cos[:], op=ALU.add)
-                nc.gpsimd.dma_start(out=out_rot[rows, col_rot : col_rot + UNIT], in_=y1_cos[:])
-                nc.gpsimd.dma_start(
-                    out=out_rot[rows, HALF + col_rot : HALF + col_rot + UNIT], in_=y1_sin[:]
-                )
+                rotated[n] = (by_cos, by_sin)
 
-        for s in range(STEPS + PASS_LAG + 1):
-            next_unit = s // UNIT_STEPS + RAW_BUFS - 1
-            if s % UNIT_STEPS == 0 and RAW_BUFS <= next_unit < UNITS:
-                load_unit(next_unit)
-            if s < STEPS:
-                transpose_step(s)
-            if 1 <= s <= STEPS:
-                quantise_step(s - 1)
-            if 0 <= s - PASS_LAG < PRODUCTS:
-                multiply(s - PASS_LAG)
-            if 0 <= s - PASS_LAG - 1 < PRODUCTS:
-                finish(s - PASS_LAG - 1)
+        def rotary_sums(n):
+            i, m = divmod(n, ROW_TILES)
+            out, col = units[i - 1][1], units[i - 1][2]
+            rows = slice(m * P, (m + 1) * P)
+            y1_cos, y1_sin = rotated[n - ROW_TILES]
+            y2_cos, y2_sin = rotated[n]
+            nc.vector.tensor_tensor(out=y1_cos[:], in0=y1_cos[:], in1=y2_sin[:], op=ALU.subtract)
+            nc.vector.tensor_tensor(out=y1_sin[:], in0=y1_sin[:], in1=y2_cos[:], op=ALU.add)
+            nc.sync.dma_start(out=out[rows, col : col + UNIT], in_=y1_cos[:])
+            nc.sync.dma_start(out=out[rows, HALF + col : HALF + col + UNIT], in_=y1_sin[:])
+
+        for c in range(CHUNKS + PASS_LAG + 1):
+            if 1 <= c and c + RAW_BUFS - 1 < CHUNKS:
+                load_chunk(c + RAW_BUFS - 1)
+            if c < CHUNKS:
+                transpose_chunk(c)
+            if c == 0:
+                finish_norm()
+            if 1 <= c <= CHUNKS:
+                quantise_chunk(c - 1)
+            if 0 <= c - PASS_LAG < PRODUCTS:
+                multiply(c - PASS_LAG)
+            emptied = c - PASS_LAG - 1
+            if 0 <= emptied < PRODUCTS:
+                empty_bank(emptied)
+            summed = emptied - SUM_LAG
+            if 0 <= summed < PRODUCTS and units[summed // ROW_TILES][3] == SECOND:
+                rotary_sums(summed)

@@ -39,7 +39,10 @@ PLAIN = 2
 
 RAW_BUFS = 6
 TABLES_AFTER = 4
+RUN = 2
 PASS_LAG = 3
+FLIP_BANKS = 5
+ACC_BANKS = 3
 SUM_LAG = 2
 
 FLOPS = 2 * S * D * 3 * DA
@@ -67,8 +70,8 @@ def tile_llamablock_pa_kernel(tc, x, w_rn1, wq, wk, wv, cos, sin, out_0, out_1, 
         first_pool = ctx.enter_context(tc.tile_pool(name="first", bufs=4))
         second_pool = ctx.enter_context(tc.tile_pool(name="second", bufs=2))
         plain_pool = ctx.enter_context(tc.tile_pool(name="plain", bufs=3))
-        flip_psum = ctx.enter_context(tc.psum_pool(name="flip", bufs=4))
-        acc_psum = ctx.enter_context(tc.psum_pool(name="acc", bufs=4))
+        flip_psum = ctx.enter_context(tc.psum_pool(name="flip", bufs=FLIP_BANKS))
+        acc_psum = ctx.enter_context(tc.psum_pool(name="acc", bufs=ACC_BANKS))
         ctx.enter_context(tc.manual_schedule())
 
         raw_of = {}
@@ -136,7 +139,7 @@ def tile_llamablock_pa_kernel(tc, x, w_rn1, wq, wk, wv, cos, sin, out_0, out_1, 
         x_words = x_sb[:].bitcast(F32)
         xg = keep.tile([P, PASSES * S * 4], F32)
         for g in range(PASSES):
-            x_t = acc_psum.tile([P, BANK], F32, tag="acc")
+            x_t = flip_psum.tile([P, BANK], F32, tag="flipped")
             for u in range(2):
                 for m in range(ROW_TILES):
                     first = m * ROW_WORDS + g * PASS_WORDS + u * P
@@ -273,8 +276,9 @@ def tile_llamablock_pa_kernel(tc, x, w_rn1, wq, wk, wv, cos, sin, out_0, out_1, 
                 finish_norm()
             if 1 <= c <= CHUNKS:
                 quantise_chunk(c - 1)
-            if 0 <= c - PASS_LAG < PRODUCTS:
-                multiply(c - PASS_LAG)
+            if 0 <= c - PASS_LAG < PRODUCTS and (c - PASS_LAG) % RUN == 0:
+                for n in range(c - PASS_LAG, c - PASS_LAG + RUN):
+                    multiply(n)
             emptied = c - PASS_LAG - 1
             if 0 <= emptied < PRODUCTS:
                 empty_bank(emptied)

@@ -37,12 +37,10 @@ FIRST = 0
 SECOND = 1
 PLAIN = 2
 
-RAW_BUFS = 6
+RAW_BUFS = 8
 TABLES_AFTER = 4
-RUN = 2
 PASS_LAG = 3
-FLIP_BANKS = 5
-ACC_BANKS = 3
+LAST_ROUNDS = 2
 SUM_LAG = 2
 
 FLOPS = 2 * S * D * 3 * DA
@@ -65,13 +63,13 @@ def tile_llamablock_pa_kernel(tc, x, w_rn1, wq, wk, wv, cos, sin, out_0, out_1, 
     with ExitStack() as ctx:
         keep = ctx.enter_context(tc.tile_pool(name="keep", bufs=1))
         raw_pool = ctx.enter_context(tc.tile_pool(name="raw", bufs=RAW_BUFS))
-        grouped_pool = ctx.enter_context(tc.tile_pool(name="grouped", bufs=3))
+        grouped_pool = ctx.enter_context(tc.tile_pool(name="grouped", bufs=4))
         mx_pool = ctx.enter_context(tc.tile_pool(name="mx", bufs=3))
         first_pool = ctx.enter_context(tc.tile_pool(name="first", bufs=4))
         second_pool = ctx.enter_context(tc.tile_pool(name="second", bufs=2))
         plain_pool = ctx.enter_context(tc.tile_pool(name="plain", bufs=3))
-        flip_psum = ctx.enter_context(tc.psum_pool(name="flip", bufs=FLIP_BANKS))
-        acc_psum = ctx.enter_context(tc.psum_pool(name="acc", bufs=ACC_BANKS))
+        flip_psum = ctx.enter_context(tc.psum_pool(name="flip", bufs=4))
+        acc_psum = ctx.enter_context(tc.psum_pool(name="acc", bufs=4))
         ctx.enter_context(tc.manual_schedule())
 
         raw_of = {}
@@ -107,8 +105,13 @@ def tile_llamablock_pa_kernel(tc, x, w_rn1, wq, wk, wv, cos, sin, out_0, out_1, 
             out=gain_rows[0 : D // (2 * P), :], in_=w_rn1.rearrange("(a c) -> a c", c=2 * P)
         )
         x_sb = keep.tile([P, ROW_TILES * D], BF16)
-        for m in range(ROW_TILES):
-            nc.sync.dma_start(out=x_sb[:, m * D : (m + 1) * D], in_=x[m * P : (m + 1) * P, :])
+        for g in range(PASSES):
+            nc.sync.dma_start(
+                out=x_sb[:, g * ROW_TILES * K_PASS : (g + 1) * ROW_TILES * K_PASS].rearrange(
+                    "p (m k) -> p m k", m=ROW_TILES
+                ),
+                in_=x[:, g * K_PASS : (g + 1) * K_PASS].rearrange("(m p) k -> p m k", p=P),
+            )
         cos_sb = keep.tile([P, ROW_TILES * HALF], BF16)
         sin_sb = keep.tile([P, ROW_TILES * HALF], BF16)
         for c in range(RAW_BUFS):
@@ -130,8 +133,8 @@ def tile_llamablock_pa_kernel(tc, x, w_rn1, wq, wk, wv, cos, sin, out_0, out_1, 
         for m in range(ROW_TILES):
             squares = keep.tile([P, D], BF16, name="squares%d" % m)
             nc.scalar.activation(
-                out=squares[:],
-                in_=x_sb[:, m * D : (m + 1) * D],
+                out=squares[:].rearrange("p (g k) -> p g k", g=PASSES),
+                in_=x_sb[:].rearrange("p (g m k) -> p m g k", g=PASSES, m=ROW_TILES)[:, m],
                 func=ACT.Square,
                 accum_out=sumsq[:, m : m + 1],
             )
@@ -139,10 +142,10 @@ def tile_llamablock_pa_kernel(tc, x, w_rn1, wq, wk, wv, cos, sin, out_0, out_1, 
         x_words = x_sb[:].bitcast(F32)
         xg = keep.tile([P, PASSES * S * 4], F32)
         for g in range(PASSES):
-            x_t = flip_psum.tile([P, BANK], F32, tag="flipped")
+            x_t = acc_psum.tile([P, BANK], F32, tag="acc")
             for u in range(2):
                 for m in range(ROW_TILES):
-                    first = m * ROW_WORDS + g * PASS_WORDS + u * P
+                    first = (g * ROW_TILES + m) * PASS_WORDS + u * P
                     nc.tensor.transpose(
                         out=x_t[:, u * S + m * P : u * S + (m + 1) * P],
                         in_=x_words[:, first : first + P],
@@ -157,9 +160,6 @@ def tile_llamablock_pa_kernel(tc, x, w_rn1, wq, wk, wv, cos, sin, out_0, out_1, 
                 op=ALU.mult,
             )
 
-        h_codes = keep.tile([P, PASSES * S], U32, align_bytes=64)
-        h_scales = keep.tile([P, PASSES * S], U8, align_bytes=64)
-
         std = keep.tile([P, ROW_TILES], F32)
         nc.scalar.activation(out=std[:], in_=sumsq[:], func=ACT.Sqrt, bias=eps[:], scale=1.0 / D)
         rstd = keep.tile([P, ROW_TILES], F32)
@@ -170,23 +170,28 @@ def tile_llamablock_pa_kernel(tc, x, w_rn1, wq, wk, wv, cos, sin, out_0, out_1, 
                 out=rstd_rep[:, m * P : (m + 1) * P], in0=ones[:], scalar1=rstd[:, m : m + 1]
             )
 
-        def finish_norm():
+        h_codes_of = {}
+        h_scales_of = {}
+
+        def finish_norm(m):
             rstd_t = acc_psum.tile([P, BANK], F32, tag="acc")
-            for m in range(ROW_TILES):
-                nc.tensor.transpose(
-                    out=rstd_t[:, m * P : (m + 1) * P],
-                    in_=rstd_rep[:, m * P : (m + 1) * P],
-                    identity=ident[:],
-                )
-            h_grouped = keep.tile([P, PASSES * S * 4], BF16, align_bytes=64)
-            for g in range(PASSES):
-                nc.vector.tensor_tensor(
-                    out=h_grouped[:, g * S * 4 : (g + 1) * S * 4].rearrange("p (s t) -> p s t", t=4),
-                    in0=xg[:, g * S * 4 : (g + 1) * S * 4].rearrange("p (s t) -> p s t", t=4),
-                    in1=rstd_t[:, 0:S].unsqueeze(2).to_broadcast([P, S, 4]),
-                    op=ALU.mult,
-                )
+            nc.tensor.transpose(
+                out=rstd_t[:, 0:P], in_=rstd_rep[:, m * P : (m + 1) * P], identity=ident[:]
+            )
+            h_grouped = keep.tile([P, PASSES * P * 4], BF16, align_bytes=64, name="h_grouped%d" % m)
+            nc.vector.tensor_tensor(
+                out=h_grouped[:].rearrange("p (g s t) -> p g s t", g=PASSES, t=4),
+                in0=xg[:].rearrange("p (g s t) -> p g s t", g=PASSES, t=4)[:, :, m * P : (m + 1) * P, :],
+                in1=rstd_t[:, 0:P]
+                .rearrange("p (o s i) -> p o s i", o=1, i=1)
+                .to_broadcast([P, PASSES, P, 4]),
+                op=ALU.mult,
+            )
+            h_codes = keep.tile([P, PASSES * P], U32, align_bytes=64, name="h_codes%d" % m)
+            h_scales = keep.tile([P, PASSES * P], U8, align_bytes=64, name="h_scales%d" % m)
             nc.vector.quantize_mx(out=h_codes[:].bitcast(FP8X4), scales=h_scales[:], in_=h_grouped[:])
+            h_codes_of[m] = h_codes
+            h_scales_of[m] = h_scales
 
         def transpose_chunk(c):
             raw_words = raw_of[c][:].bitcast(F32)
@@ -226,12 +231,12 @@ def tile_llamablock_pa_kernel(tc, x, w_rn1, wq, wk, wv, cos, sin, out_0, out_1, 
             i, m = divmod(n, ROW_TILES)
             acc = acc_psum.tile([P, BANK], F32, tag="acc")
             for g in range(PASSES):
-                rows = slice(g * S + m * P, g * S + (m + 1) * P)
+                rows = slice(g * P, (g + 1) * P)
                 cols = slice(g * UNIT, (g + 1) * UNIT)
                 nc.tensor.matmul_mx(
                     out=acc[:],
-                    lhsT=h_codes[:, rows].bitcast(FP8X4),
-                    lhsT_scale=h_scales[:, rows],
+                    lhsT=h_codes_of[m][:, rows].bitcast(FP8X4),
+                    lhsT_scale=h_scales_of[m][:, rows],
                     rhs=codes_of[i][:, cols].bitcast(FP8X4),
                     rhs_scale=scales_of[i][:, cols],
                     start=(g == 0),
@@ -267,18 +272,20 @@ def tile_llamablock_pa_kernel(tc, x, w_rn1, wq, wk, wv, cos, sin, out_0, out_1, 
             nc.sync.dma_start(out=out[rows, col : col + UNIT], in_=y1_cos[:])
             nc.sync.dma_start(out=out[rows, HALF + col : HALF + col + UNIT], in_=y1_sin[:])
 
+        multiplied = 0
         for c in range(CHUNKS + PASS_LAG + 1):
             if 1 <= c and c + RAW_BUFS - 1 < CHUNKS:
                 load_chunk(c + RAW_BUFS - 1)
             if c < CHUNKS:
                 transpose_chunk(c)
-            if c == 0:
-                finish_norm()
             if 1 <= c <= CHUNKS:
                 quantise_chunk(c - 1)
-            if 0 <= c - PASS_LAG < PRODUCTS and (c - PASS_LAG) % RUN == 0:
-                for n in range(c - PASS_LAG, c - PASS_LAG + RUN):
-                    multiply(n)
+            if c % UNIT_CHUNKS == 0 and c // UNIT_CHUNKS < ROW_TILES:
+                finish_norm(c // UNIT_CHUNKS)
+            due = c - PASS_LAG + 1 + (1 if c >= CHUNKS - LAST_ROUNDS else 0)
+            for n in range(multiplied, min(due, PRODUCTS)):
+                multiply(n)
+                multiplied = n + 1
             emptied = c - PASS_LAG - 1
             if 0 <= emptied < PRODUCTS:
                 empty_bank(emptied)

from contextlib import ExitStack

import concourse.mybir as mybir
from concourse.masks import make_identity

BF16 = mybir.dt.bfloat16
F32 = mybir.dt.float32
U32 = mybir.dt.uint32
U8 = mybir.dt.uint8
FP8X4 = mybir.dt.float8_e4m3fn_x4
ACT = mybir.ActivationFunctionType
ALU = mybir.AluOpType

P = 128
S = 256
D = 2048
DA = 2048
HALF = DA // 2
EPS = 1.1920929e-07

ROW_TILES = S // P
K_PASS = 4 * P
PASSES = D // K_PASS
PASS_WORDS = K_PASS // 2
ROW_WORDS = D // 2
BANK = 512

UNIT = 512
UNITS = 3 * DA // UNIT
PRODUCTS = UNITS * ROW_TILES
CHUNK = 256
CHUNK_TILES = CHUNK // P
UNIT_CHUNKS = UNIT // CHUNK
CHUNKS = UNITS * UNIT_CHUNKS

FIRST = 0
SECOND = 1
PLAIN = 2

RAW_BUFS = 8
TABLES_AFTER = 4
PASS_LAG = 3
LAST_ROUNDS = 2
SUM_LAG = 2

FLOPS = 2 * S * D * 3 * DA


def tile_llamablock_pa_kernel(tc, x, w_rn1, wq, wk, wv, cos, sin, out_0, out_1, out_2):
    nc = tc.nc

    def rotary_pair(w, out, col):
        return [(w, out, col, FIRST), (w, out, HALF + col, SECOND)]

    def plain(block):
        return [(wv, out_2, block * UNIT, PLAIN)]

    units = (
        rotary_pair(wq, out_0, 0) + plain(0) + rotary_pair(wq, out_0, UNIT) + plain(1)
        + rotary_pair(wk, out_1, 0) + rotary_pair(wk, out_1, UNIT) + plain(2) + plain(3)
    )

    with ExitStack() as ctx:
        keep = ctx.enter_context(tc.tile_pool(name="keep", bufs=1))
        raw_pool = ctx.enter_context(tc.tile_pool(name="raw", bufs=RAW_BUFS))
        grouped_pool = ctx.enter_context(tc.tile_pool(name="grouped", bufs=4))
        mx_pool = ctx.enter_context(tc.tile_pool(name="mx", bufs=3))
        first_pool = ctx.enter_context(tc.tile_pool(name="first", bufs=4))
        second_pool = ctx.enter_context(tc.tile_pool(name="second", bufs=2))
        plain_pool = ctx.enter_context(tc.tile_pool(name="plain", bufs=3))
        flip_psum = ctx.enter_context(tc.psum_pool(name="flip", bufs=4))
        acc_psum = ctx.enter_context(tc.psum_pool(name="acc", bufs=4))
        ctx.enter_context(tc.manual_schedule())

        raw_of = {}
        grouped_of = {}
        codes_of = {}
        scales_of = {}
        acc_of = {}
        rotated = {}

        def load_chunk(c):
            i, part = divmod(c, UNIT_CHUNKS)
            w_dram = units[i][0]
            row = units[i][2] + part * CHUNK
            raw = raw_pool.tile([P, CHUNK_TILES * D], BF16)
            nc.sync.dma_start(
                out=raw[:].rearrange("p (t k) -> p t k", t=CHUNK_TILES),
                in_=w_dram[row : row + CHUNK, :].rearrange("(t p) k -> p t k", p=P),
            )
            raw_of[c] = raw

        gain_rows = keep.tile([P, 2 * P], BF16)
        nc.vector.memset(gain_rows[:], 0.0)
        eps = keep.tile([P, 1], F32)
        nc.vector.memset(eps[:], EPS)
        ones = keep.tile([P, P], F32)
        nc.vector.memset(ones[:], 1.0)
        ident = keep.tile([P, P], F32)
        make_identity(nc, ident[:])
        warm = keep.tile([P, 1], F32)
        nc.scalar.activation(out=warm[:], in_=eps[:], func=ACT.Sqrt)

        nc.sync.dma_start(
            out=gain_rows[0 : D // (2 * P), :], in_=w_rn1.rearrange("(a c) -> a c", c=2 * P)
        )
        x_sb = keep.tile([P, ROW_TILES * D], BF16)
        for g in range(PASSES):
            nc.sync.dma_start(
                out=x_sb[:, g * ROW_TILES * K_PASS : (g + 1) * ROW_TILES * K_PASS].rearrange(
                    "p (m k) -> p m k", m=ROW_TILES
                ),
                in_=x[:, g * K_PASS : (g + 1) * K_PASS].rearrange("(m p) k -> p m k", p=P),
            )
        cos_sb = keep.tile([P, ROW_TILES * HALF], BF16)
        sin_sb = keep.tile([P, ROW_TILES * HALF], BF16)
        for c in range(RAW_BUFS):
            load_chunk(c)
            if c == TABLES_AFTER:
                for table, table_sb in ((cos, cos_sb), (sin, sin_sb)):
                    nc.sync.dma_start(
                        out=table_sb[:].rearrange("p (m j) -> p m j", m=ROW_TILES),
                        in_=table.rearrange("(m p) j -> p m j", p=P),
                    )

        gain_t = acc_psum.tile([P, BANK], F32, tag="acc")
        nc.tensor.transpose(out=gain_t[:, 0:P], in_=gain_rows[:].bitcast(F32), identity=ident[:])
        gain4 = keep.tile([P, 2 * PASSES], F32)
        nc.vector.tensor_copy(out=gain4[:], in_=gain_t[:, 0 : 2 * PASSES])
        gain4_bf = gain4[:].bitcast(BF16)

        sumsq = keep.tile([P, ROW_TILES], F32)
        for m in range(ROW_TILES):
            squares = keep.tile([P, D], BF16, name="squares%d" % m)
            nc.scalar.activation(
                out=squares[:].rearrange("p (g k) -> p g k", g=PASSES),
                in_=x_sb[:].rearrange("p (g m k) -> p m g k", g=PASSES, m=ROW_TILES)[:, m],
                func=ACT.Square,
                accum_out=sumsq[:, m : m + 1],
            )

        x_words = x_sb[:].bitcast(F32)
        xg = keep.tile([P, PASSES * S * 4], F32)
        for g in range(PASSES):
            x_t = acc_psum.tile([P, BANK], F32, tag="acc")
            for u in range(2):
                for m in range(ROW_TILES):
                    first = (g * ROW_TILES + m) * PASS_WORDS + u * P
                    nc.tensor.transpose(
                        out=x_t[:, u * S + m * P : u * S + (m + 1) * P],
                        in_=x_words[:, first : first + P],
                        identity=ident[:],
                    )
            nc.vector.tensor_tensor(
                out=xg[:, g * S * 4 : (g + 1) * S * 4].rearrange("p (s u e) -> p s u e", u=2, e=2),
                in0=x_t[:].bitcast(BF16).rearrange("p (u s e) -> p s u e", u=2, e=2),
                in1=gain4_bf[:, 4 * g : 4 * g + 4]
                .rearrange("p (o u e) -> p o u e", o=1, u=2)
                .to_broadcast([P, S, 2, 2]),
                op=ALU.mult,
            )

        std = keep.tile([P, ROW_TILES], F32)
        nc.scalar.activation(out=std[:], in_=sumsq[:], func=ACT.Sqrt, bias=eps[:], scale=1.0 / D)
        rstd = keep.tile([P, ROW_TILES], F32)
        nc.vector.reciprocal(out=rstd[:], in_=std[:])
        rstd_rep = keep.tile([P, S], F32)
        for m in range(ROW_TILES):
            nc.vector.tensor_scalar_mul(
                out=rstd_rep[:, m * P : (m + 1) * P], in0=ones[:], scalar1=rstd[:, m : m + 1]
            )

        h_codes_of = {}
        h_scales_of = {}

        def finish_norm(m):
            rstd_t = acc_psum.tile([P, BANK], F32, tag="acc")
            nc.tensor.transpose(
                out=rstd_t[:, 0:P], in_=rstd_rep[:, m * P : (m + 1) * P], identity=ident[:]
            )
            h_grouped = keep.tile([P, PASSES * P * 4], BF16, align_bytes=64, name="h_grouped%d" % m)
            nc.vector.tensor_tensor(
                out=h_grouped[:].rearrange("p (g s t) -> p g s t", g=PASSES, t=4),
                in0=xg[:].rearrange("p (g s t) -> p g s t", g=PASSES, t=4)[:, :, m * P : (m + 1) * P, :],
                in1=rstd_t[:, 0:P]
                .rearrange("p (o s i) -> p o s i", o=1, i=1)
                .to_broadcast([P, PASSES, P, 4]),
                op=ALU.mult,
            )
            h_codes = keep.tile([P, PASSES * P], U32, align_bytes=64, name="h_codes%d" % m)
            h_scales = keep.tile([P, PASSES * P], U8, align_bytes=64, name="h_scales%d" % m)
            nc.vector.quantize_mx(out=h_codes[:].bitcast(FP8X4), scales=h_scales[:], in_=h_grouped[:])
            h_codes_of[m] = h_codes
            h_scales_of[m] = h_scales

        def transpose_chunk(c):
            raw_words = raw_of[c][:].bitcast(F32)
            grouped = grouped_pool.tile([P, PASSES * CHUNK * 4], BF16, align_bytes=64)
            grouped_words = grouped[:].bitcast(F32).rearrange("p (g n u) -> p g n u", g=PASSES, u=2)
            for g in range(PASSES):
                flipped = flip_psum.tile([P, BANK], F32)
                for u in range(2):
                    for t in range(CHUNK_TILES):
                        first = t * ROW_WORDS + g * PASS_WORDS + u * P
                        nc.tensor.transpose(
                            out=flipped[:, u * CHUNK + t * P : u * CHUNK + (t + 1) * P],
                            in_=raw_words[:, first : first + P],
                            identity=ident[:],
                        )
                nc.scalar.copy(
                    out=grouped_words[:, g], in_=flipped[:].rearrange("p (u n) -> p n u", u=2)
                )
            grouped_of[c] = grouped

        def quantise_chunk(c):
            i, part = divmod(c, UNIT_CHUNKS)
            if part == 0:
                codes = mx_pool.tile([P, PASSES * UNIT], U32, align_bytes=64)
                scales = mx_pool.tile([P, PASSES * UNIT], U8, align_bytes=64)
                codes_of[i] = codes
                scales_of[i] = scales
            for g in range(PASSES):
                cols = slice(g * UNIT + part * CHUNK, g * UNIT + (part + 1) * CHUNK)
                nc.vector.quantize_mx(
                    out=codes_of[i][:, cols].bitcast(FP8X4),
                    scales=scales_of[i][:, cols],
                    in_=grouped_of[c][:, g * CHUNK * 4 : (g + 1) * CHUNK * 4],
                )

        def multiply(n):
            i, m = divmod(n, ROW_TILES)
            acc = acc_psum.tile([P, BANK], F32, tag="acc")
            for g in range(PASSES):
                rows = slice(g * P, (g + 1) * P)
                cols = slice(g * UNIT, (g + 1) * UNIT)
                nc.tensor.matmul_mx(
                    out=acc[:],
                    lhsT=h_codes_of[m][:, rows].bitcast(FP8X4),
                    lhsT_scale=h_scales_of[m][:, rows],
                    rhs=codes_of[i][:, cols].bitcast(FP8X4),
                    rhs_scale=scales_of[i][:, cols],
                    start=(g == 0),
                    stop=(g == PASSES - 1),
                )
            acc_of[n] = acc

        def empty_bank(n):
            i, m = divmod(n, ROW_TILES)
            out, col, kind = units[i][1], units[i][2], units[i][3]
            acc = acc_of[n]
            if kind == PLAIN:
                v_sb = plain_pool.tile([P, UNIT], F32)
                nc.scalar.copy(out=v_sb[:], in_=acc[:])
                nc.sync.dma_start(out=out[m * P : (m + 1) * P, col : col + UNIT], in_=v_sb[:])
            else:
                pool = first_pool if kind == FIRST else second_pool
                table_cols = slice(m * HALF + col % HALF, m * HALF + col % HALF + UNIT)
                by_cos = pool.tile([P, UNIT], F32)
                by_sin = pool.tile([P, UNIT], F32)
                nc.vector.tensor_tensor(out=by_cos[:], in0=acc[:], in1=cos_sb[:, table_cols], op=ALU.mult)
                nc.vector.tensor_tensor(out=by_sin[:], in0=acc[:], in1=sin_sb[:, table_cols], op=ALU.mult)
                rotated[n] = (by_cos, by_sin)

        def rotary_sums(n):
            i, m = divmod(n, ROW_TILES)
            out, col = units[i - 1][1], units[i - 1][2]
            rows = slice(m * P, (m + 1) * P)
            y1_cos, y1_sin = rotated[n - ROW_TILES]
            y2_cos, y2_sin = rotated[n]
            nc.vector.tensor_tensor(out=y1_cos[:], in0=y1_cos[:], in1=y2_sin[:], op=ALU.subtract)
            nc.vector.tensor_tensor(out=y1_sin[:], in0=y1_sin[:], in1=y2_cos[:], op=ALU.add)
            nc.sync.dma_start(out=out[rows, col : col + UNIT], in_=y1_cos[:])
            nc.sync.dma_start(out=out[rows, HALF + col : HALF + col + UNIT], in_=y1_sin[:])

        multiplied = 0
        for c in range(CHUNKS + PASS_LAG + 1):
            if 1 <= c and c + RAW_BUFS - 1 < CHUNKS:
                load_chunk(c + RAW_BUFS - 1)
            if c < CHUNKS:
                transpose_chunk(c)
            if 1 <= c <= CHUNKS:
                quantise_chunk(c - 1)
            if c % UNIT_CHUNKS == 0 and c // UNIT_CHUNKS < ROW_TILES:
                finish_norm(c // UNIT_CHUNKS)
            due = c - PASS_LAG + 1 + (1 if c >= CHUNKS - LAST_ROUNDS else 0)
            for n in range(multiplied, min(due, PRODUCTS)):
                multiply(n)
                multiplied = n + 1
            emptied = c - PASS_LAG - 1
            if 0 <= emptied < PRODUCTS:
                empty_bank(emptied)
            summed = emptied - SUM_LAG
            if 0 <= summed < PRODUCTS and units[summed // ROW_TILES][3] == SECOND:
                rotary_sums(summed)
